import numpy as np
import ml_dtypes


def mxq(x, axis, fmt="e4m3"):
    dtype, down = {"e4m3": (ml_dtypes.float8_e4m3fn, 7), "e5m2": (ml_dtypes.float8_e5m2, 14)}[fmt]
    v = np.moveaxis(np.asarray(x, np.float32).astype(ml_dtypes.bfloat16).astype(np.float64), axis, -1)
    blocks = v.reshape(v.shape[:-1] + (-1, 32))
    amax = np.abs(blocks).max(-1, keepdims=True)
    byte = np.maximum(np.where(amax > 0, np.frexp(amax)[1] - 1 + 127, 0) - down, 1)
    scale = np.exp2(byte - 127.0)
    codes = (blocks / scale).astype(np.float32).astype(dtype).astype(np.float64)
    return np.moveaxis((codes * scale).reshape(v.shape), -1, axis)


WIDE = False


def mx_kscale(k):
    if not WIDE:
        return np.ones(k)
    levels = np.array([10, -10, 5, -5, 0])
    a = np.random.permutation(np.resize(levels, k // 512 * 4)).reshape(k // 512, 4)
    idx = np.arange(k)
    return np.exp2(a[idx // 512, idx % 128 // 32])


BF16 = ml_dtypes.bfloat16


def bf(x):
    return np.asarray(x, np.float32).astype(BF16)


def f64(x):
    return np.asarray(x).astype(np.float64)


E2M1 = np.array([0.0, 0.5, 1.0, 1.5, 2.0, 3.0, 4.0, 6.0, -0.0, -0.5, -1.0, -1.5, -2.0, -3.0, -4.0, -6.0])


def pack_weight(w, fmt):
    k, n = w.shape
    w = f64(bf(w)).reshape(k // 32, 32, n)
    amax = np.abs(w).max(1)
    if fmt == "e4m3":
        byte = np.frexp(amax)[1] - 1 + 127 - 7
    else:
        mant, ex = np.frexp(amax / 6.0)
        byte = np.where(mant > 0.5, ex, ex - 1) + 127
    byte = np.clip(np.where(amax > 0, byte, 1), 1, 254)
    scaled = (w * np.exp2(127.0 - byte)[:, None, :]).reshape(k, n).astype(np.float32)
    by_word = np.ascontiguousarray(scaled.reshape(k // 512, 128, 4, n).transpose(0, 1, 3, 2))
    if fmt == "e4m3":
        words = by_word.astype(ml_dtypes.float8_e4m3fn).view(np.uint8)
    else:
        c = by_word.astype(ml_dtypes.float4_e2m1fn).view(np.uint8) & 0xF
        words = c[..., 0::2] | (c[..., 1::2] << 4)
    return np.ascontiguousarray(words), np.ascontiguousarray(byte.astype(np.uint8).reshape(k // 512, 16, n))


def unpack_weight(words, scales, fmt):
    g, p, n, _ = words.shape
    if fmt == "e4m3":
        vals = np.ascontiguousarray(words).view(ml_dtypes.float8_e4m3fn).astype(np.float64)
    else:
        nib = np.empty((g, p, n, 4), np.uint8)
        nib[..., 0::2] = words & 0xF
        nib[..., 1::2] = words >> 4
        vals = E2M1[nib]
    vals = vals * np.repeat(np.exp2(scales.astype(np.float64) - 127.0), 8, axis=1)[..., None]
    return vals.transpose(0, 1, 3, 2).reshape(g * 512, n)

def pack4(w):
    words, scales = pack_weight(w, "e2m1")
    return words.reshape(words.shape[0], 128, -1), scales


def unpack4(words, scales):
    return unpack_weight(words.reshape(words.shape[0], 128, -1, 2), scales, "e2m1")


B, IN, OUT, G = 512, 1024, 512, 20


def silu(v):
    with np.errstate(over="ignore"):
        return v / (1.0 + np.exp(-v))


def setup_inputs():
    bound = 1.0 / np.sqrt(IN)
    s = mx_kscale(IN)
    c = np.maximum(s, 1.0)
    x = bf(np.random.standard_normal((B, IN)) * s)
    base_words, base_scales = pack4((np.random.uniform(-bound, bound, (OUT, IN)) / s).T)
    return {"x": x,
            "base_weight_words": base_words,
            "base_weight_scales": base_scales,
            "spline_weight": bf(0.05 * np.random.standard_normal((OUT, IN, G)) / c[None, :, None]),
            "spline_scale": bf(0.1 * (1.0 + 0.1 * np.random.standard_normal((OUT, 1, 1)))),
            "grid": bf(np.linspace(-2.0, 2.0, G))}


def reference(x, base_weight_words, base_weight_scales, spline_weight, spline_scale, grid):
    x, spline_weight = f64(x), f64(spline_weight)
    spline_scale, grid = f64(spline_scale), f64(grid)
    base_out = mxq(silu(x), 1, "e4m3") @ unpack4(base_weight_words, base_weight_scales)
    basis = np.maximum(x[:, :, None] - grid[None, None, :], 0.0)
    scaled_w = spline_weight * spline_scale
    basis_f = basis.transpose(0, 2, 1).reshape(basis.shape[0], -1)
    w_f = scaled_w.transpose(0, 2, 1).reshape(scaled_w.shape[0], -1)
    spline_out = mxq(basis_f, 1, "e4m3") @ mxq(w_f, 1, "e4m3").T
    return base_out + spline_out

@@ -1,0 +1,394 @@
+from contextlib import ExitStack
+
+import concourse.mybir as mybir
+from concourse.masks import make_identity
+
+FLOPS = 2 * 512 * 512 * (20 * 1024 + 1024)
+
+BF16 = mybir.dt.bfloat16
+F32 = mybir.dt.float32
+I32 = mybir.dt.int32
+U8 = mybir.dt.uint8
+U32 = mybir.dt.uint32
+FP8X4 = mybir.dt.float8_e4m3fn_x4
+FP4X4 = mybir.dt.float4_e2m1fn_x4
+ALU = mybir.AluOpType
+ACT = mybir.ActivationFunctionType
+AX = mybir.AxisListType
+
+P = 128
+GROUPS = ((0, 0, 1), (0, 1, 1), (0, 2, 2), (1, 0, 2), (1, 2, 2))
+WN_BUFS = 8
+
+
+def weave(*weighted):
+    keyed = []
+    for li, (span, items) in enumerate(weighted):
+        for k, item in enumerate(items):
+            keyed.append(((k + 0.5) * span / len(items), li, k, item))
+    return [entry[3] for entry in sorted(keyed, key=lambda e: (e[0], e[1], e[2]))]
+
+
+def tile_relukanlayer_kernel(
+    tc, x, base_weight_words, base_weight_scales, spline_weight, spline_scale, grid, out
+):
+    nc = tc.nc
+    with ExitStack() as ctx:
+        ctx.enter_context(tc.manual_schedule())
+        const = ctx.enter_context(tc.tile_pool(name="const", bufs=1))
+        wn_pool = ctx.enter_context(tc.tile_pool(name="wn", bufs=WN_BUFS))
+        wp_pool = ctx.enter_context(tc.tile_pool(name="wp", bufs=16))
+        wbf_pool = ctx.enter_context(tc.tile_pool(name="wbf", bufs=8))
+        wq_pool = ctx.enter_context(tc.tile_pool(name="wq", bufs=3))
+        bas_pool = ctx.enter_context(tc.tile_pool(name="bas", bufs=3))
+        bq_pool = ctx.enter_context(tc.tile_pool(name="bq", bufs=2))
+        res_pool = ctx.enter_context(tc.tile_pool(name="res", bufs=2))
+        acc_pool = ctx.enter_context(tc.psum_pool(name="acc", bufs=1))
+        tp_pool = ctx.enter_context(tc.psum_pool(name="tp", bufs=4))
+
+        w_v = spline_weight.rearrange("(op ob) (c t r) g -> ob c op t (r g)", ob=16, c=2, t=4)
+        x_v = x.rearrange("(m p) i -> p m i", p=P)
+        scr = out.rearrange("(c r a) n -> c r (a n)", c=2, a=2)
+
+        tiles = [(gi, ob) for gi in range(len(GROUPS)) for ob in range(16)]
+        runs = [(gi, h, cl2) for gi, grp in enumerate(GROUPS) for h in range(2) for cl2 in range(grp[2])]
+        n_runs = len(runs)
+        pre_sched = {}
+        for r, (gi, h, cl2) in enumerate(runs):
+            if cl2 != 0:
+                continue
+            first = 16 * gi + 8 * h
+            if GROUPS[gi][2] == 1:
+                pre_sched[r - 2] = list(range(first, first + 8))
+            else:
+                pre_sched[r - 2] = list(range(first, first + 4))
+                pre_sched[r - 1] = list(range(first + 4, first + 8))
+
+        ident_bf = const.tile([P, P], BF16, name="ident_bf")
+        ident_f = const.tile([P, P], F32, name="ident_f")
+        s_bf = const.tile([P, 16], BF16, name="s_bf")
+        s_f = const.tile([P, 16], F32, name="s_f")
+        gridb = const.tile([P, 20], BF16, name="gridb")
+        mask4 = const.tile([P, 4], F32, name="mask4")
+        gm = const.tile([P, 5, 4], F32, name="gm")
+        grid_f = const.tile([P, 5], F32, name="grid_f")
+        zero = const.tile([P, 2], F32, name="zero")
+        warm = const.tile([P, 2], F32, name="warm")
+        w4 = const.tile([P, 2, 1024], U8, name="w4", align_bytes=64)
+        w4s = const.tile([P, 2, 512], U8, name="w4s", align_bytes=64)
+        silq = const.tile([P, 2, 512], U32, name="silq", align_bytes=64)
+        sils = const.tile([P, 2, 512], U8, name="sils", align_bytes=64)
+        base_sb = const.tile([P, 4, 512], F32, name="base_sb")
+        xn = const.tile([P, 4, 1024], BF16, name="xn")
+        xt4 = const.tile([P, 2, 512, 4], BF16, name="xt4")
+        sil = const.tile([P, 2, 512, 4], BF16, name="sil", align_bytes=64)
+        xrep = [const.tile([P, 2048], BF16, name="xrep%d" % s) for s in range(8)]
+        acc = [acc_pool.tile([P, 512], F32, name="acc%d" % mt) for mt in range(4)]
+
+        wn_t = {}
+        after_load = {}
+        wp_t = {}
+        wbf_t = {}
+        wq_t = {}
+        bas_t = {}
+        bq_t = {}
+
+        def load_w(n):
+            if n >= len(tiles):
+                return
+            gi, ob = tiles[n]
+            c, cl0, ncl = GROUPS[gi]
+            wn = wn_pool.tile([P, 1280], BF16, name="wn", tag="wn")
+            nc.sync.dma_start(out=wn[:, : 640 * ncl], in_=w_v[ob, c][:, :, 640 * cl0 : 640 * (cl0 + ncl)])
+            wn_t[n] = wn
+            for extra in after_load.get(n, []):
+                extra()
+
+        def pre_views(n):
+            ncl = GROUPS[tiles[n][0]][2]
+            src = wn_t[n][:, : 640 * ncl].rearrange("q (i a b) -> q a i b", a=5, b=4)
+            dst = wp_t[n][:, : 640 * ncl].rearrange("q (a i b) -> q a i b", a=5, b=4)
+            return src, dst
+
+        def pre_a(n):
+            wp_t[n] = wp_pool.tile([P, 1280], BF16, name="wp", tag="wp")
+            src, dst = pre_views(n)
+            ob = tiles[n][1]
+            nc.vector.tensor_scalar(
+                out=dst[:, 0:4], in0=src[:, 0:4], scalar1=s_f[:, ob : ob + 1], scalar2=None, op0=ALU.mult
+            )
+
+        def pre_b_vector(n):
+            src, dst = pre_views(n)
+            ob = tiles[n][1]
+            nc.vector.tensor_scalar(
+                out=dst[:, 4], in0=src[:, 4], scalar1=s_f[:, ob : ob + 1], scalar2=None, op0=ALU.mult
+            )
+
+        def pre_b_scalar(n):
+            src, dst = pre_views(n)
+            ob = tiles[n][1]
+            nc.scalar.activation(out=dst[:, 4], in_=src[:, 4], func=ACT.Copy, scale=s_f[:, ob : ob + 1])
+
+        def slice_of(r):
+            gi, h, cl2 = runs[r]
+            return 4 * GROUPS[gi][0] + GROUPS[gi][1] + cl2
+
+        def half_run(r):
+            gi, h, cl2 = runs[r]
+            ni = 32 * GROUPS[gi][2]
+            for gq in range(5):
+                tp = tp_pool.tile([P, 1024], BF16, name="tp", tag="tp")
+                off = gq * ni * 4 + cl2 * P
+                for j in range(8):
+                    nc.tensor.transpose(
+                        tp[:, P * j : P * (j + 1)], wp_t[16 * gi + 8 * h + j][:, off : off + P], ident_bf[:]
+                    )
+                wbf = wbf_pool.tile([P, 1024], BF16, name="wbf", tag="wbf", align_bytes=64)
+                nc.scalar.copy(out=wbf[:], in_=tp[:])
+                wbf_t[(r, gq)] = wbf
+
+        def quant_w(r, gq):
+            h = runs[r][1]
+            s = slice_of(r)
+            if s not in wq_t:
+                wq_t[s] = (
+                    wq_pool.tile([P, 5, 512], U32, name="wq", tag="wq", align_bytes=64),
+                    wq_pool.tile([P, 5, 512], U8, name="wsc", tag="wsc", align_bytes=64),
+                )
+            codes, scales = wq_t[s]
+            nc.vector.quantize_mx(
+                out=codes[:, gq, 256 * h : 256 * (h + 1)].bitcast(FP8X4),
+                scales=scales[:, gq, 256 * h : 256 * (h + 1)],
+                in_=wbf_t[(r, gq)][:],
+            )
+
+        def basis(s, gq):
+            bas = bas_pool.tile([P, 2048], BF16, name="bas", tag="bas", align_bytes=64)
+            nc.vector.tensor_scalar(
+                out=bas[:],
+                in0=xrep[s][:],
+                scalar1=grid_f[:, gq : gq + 1],
+                scalar2=0.0,
+                op0=ALU.subtract,
+                op1=ALU.max,
+            )
+            bas_t[(s, gq)] = bas
+
+        def quant_b(s, gq):
+            if s not in bq_t:
+                bq_t[s] = (
+                    bq_pool.tile([P, 5, 512], U32, name="bq", tag="bq", align_bytes=64),
+                    bq_pool.tile([P, 5, 512], U8, name="bsc", tag="bsc", align_bytes=64),
+                )
+            codes, scales = bq_t[s]
+            nc.vector.quantize_mx(out=codes[:, gq, :].bitcast(FP8X4), scales=scales[:, gq, :], in_=bas_t[(s, gq)][:])
+
+        def mx_pass(s, gq, mt):
+            nc.tensor.matmul_mx(
+                out=acc[mt][:],
+                lhsT=bq_t[s][0][:, gq, P * mt : P * (mt + 1)].bitcast(FP8X4),
+                lhsT_scale=bq_t[s][1][:, gq, P * mt : P * (mt + 1)],
+                rhs=wq_t[s][0][:, gq, :].bitcast(FP8X4),
+                rhs_scale=wq_t[s][1][:, gq, :],
+                start=(s == 0 and gq == 0),
+                stop=(s == 7 and gq == 4),
+            )
+
+        def gqs_of(m):
+            return (0, 1, 2) if m % 2 == 0 else (3, 4)
+
+        def basis_items(m):
+            s = m // 2
+            gqs = gqs_of(m)
+            items = [lambda g=gqs[0]: basis(s, g)]
+            for k in range(1, len(gqs)):
+                items.append(lambda g=gqs[k]: basis(s, g))
+                items.append(lambda g=gqs[k - 1]: quant_b(s, g))
+            items.append(lambda g=gqs[-1]: quant_b(s, g))
+            return items
+
+        def load_xrep(s):
+            c, cl = s // 4, s % 4
+            nc.sync.dma_start(
+                out=xrep[s][:].bitcast(F32),
+                in_=scr[c][32 * cl : 32 * (cl + 1), :].unsqueeze(1).to_broadcast([32, 4, 1024]),
+            )
+
+        def x_transposes(c):
+            for mp in range(2):
+                tp = tp_pool.tile([P, 1024], BF16, name="tp", tag="tp")
+                for m2 in range(2):
+                    for t in range(4):
+                        k = 4 * m2 + t
+                        nc.tensor.transpose(
+                            tp[:, P * k : P * (k + 1)],
+                            xn[:, 2 * mp + m2, 512 * c + P * t : 512 * c + P * (t + 1)],
+                            ident_bf[:],
+                        )
+                nc.scalar.copy(
+                    out=xt4[:, c, 256 * mp : 256 * (mp + 1), :].rearrange("p (m b) t -> p m b t", m=2),
+                    in_=tp[:].rearrange("p (m t b) -> p m b t", m=2, t=4),
+                )
+
+        def store_xt(c):
+            nc.sync.dma_start(out=scr[c], in_=xt4[:, c].rearrange("p b t -> p (b t)").bitcast(F32))
+
+        def base_transposes(c):
+            for mp in range(2):
+                tpf = tp_pool.tile([P, 512], F32, name="tpf", tag="tp")
+                for m2 in range(2):
+                    words = xn[:, 2 * mp + m2, :].bitcast(F32)
+                    for u in range(2):
+                        k = 2 * m2 + u
+                        nc.tensor.transpose(
+                            tpf[:, P * k : P * (k + 1)], words[:, 256 * c + u : 256 * (c + 1) : 2], ident_f[:]
+                        )
+                for m2 in range(2):
+                    mt = 2 * mp + m2
+                    nc.scalar.activation(
+                        out=sil[:, c, P * mt : P * (mt + 1), :].rearrange("p b (u e) -> p b u e", u=2),
+                        in_=tpf[:, 256 * m2 : 256 * (m2 + 1)].bitcast(BF16).rearrange("p (u b e) -> p b u e", u=2, e=2),
+                        func=ACT.Silu,
+                    )
+
+        def base_quant(c):
+            nc.vector.quantize_mx(
+                out=silq[:, c, :].bitcast(FP8X4),
+                scales=sils[:, c, :],
+                in_=sil[:, c].rearrange("p b t -> p (b t)"),
+            )
+
+        def base_matmuls():
+            for mt in range(4):
+                pb = tp_pool.tile([P, 512], F32, name="pb", tag="tp")
+                for c in range(2):
+                    nc.tensor.matmul_mx(
+                        out=pb[:],
+                        lhsT=silq[:, c, P * mt : P * (mt + 1)].bitcast(FP8X4),
+                        lhsT_scale=sils[:, c, P * mt : P * (mt + 1)],
+                        rhs=w4[:, c, :].bitcast(FP4X4),
+                        rhs_scale=w4s[:, c, :],
+                        start=(c == 0),
+                        stop=(c == 1),
+                    )
+                if mt % 2 == 0:
+                    nc.scalar.copy(out=base_sb[:, mt, :], in_=pb[:])
+                else:
+                    nc.vector.tensor_copy(out=base_sb[:, mt, :], in_=pb[:])
+
+        def finish(mt):
+            res = res_pool.tile([P, 512], F32, name="res", tag="res")
+            nc.vector.tensor_tensor(
+                out=res[:].rearrange("b (op ob) -> b op ob", ob=16),
+                in0=acc[mt][:].rearrange("b (ob op) -> b op ob", ob=16),
+                in1=base_sb[:, mt, :].rearrange("b (op ob) -> b op ob", ob=16),
+                op=ALU.add,
+            )
+            nc.sync.dma_start(out=out[P * mt : P * (mt + 1), :], in_=res[:])
+
+        def load_x(c):
+            nc.sync.dma_start(out=xn[:, :, 512 * c : 512 * (c + 1)], in_=x_v[:, :, 512 * c : 512 * (c + 1)])
+
+        def load_base():
+            nc.sync.dma_start(out=gridb[:], in_=grid.partition_broadcast(P))
+            nc.sync.dma_start(out=w4[:].bitcast(I32), in_=base_weight_words.bitcast(I32).rearrange("g p n -> p g n"))
+            for q in range(4):
+                nc.sync.dma_start(
+                    out=w4s[32 * q : 32 * q + 4].bitcast(I32),
+                    in_=base_weight_scales.bitcast(I32)[:, 4 * q : 4 * q + 4, :].rearrange("g r n -> r g n"),
+                )
+
+        after_load[15] = [lambda: store_xt(0), lambda: load_x(1)]
+        after_load[23] = [lambda: load_xrep(0)]
+        after_load[27] = [load_base]
+        after_load[31] = [lambda: load_xrep(1)]
+        after_load[35] = [lambda: store_xt(1), lambda: load_xrep(2)]
+        after_load[39] = [lambda: load_xrep(3)]
+        after_load[43] = [lambda: load_xrep(4)]
+        after_load[47] = [lambda: load_xrep(5)]
+        after_load[51] = [lambda: load_xrep(6)]
+        after_load[55] = [lambda: load_xrep(7)]
+
+        load_x(0)
+        nc.sync.dma_start(
+            out=s_bf[:],
+            in_=spline_scale.rearrange("(op ob) a b -> op (ob a b)", ob=16).unsqueeze(1).to_broadcast([32, 4, 16]),
+        )
+        make_identity(nc, ident_bf[:])
+        make_identity(nc, ident_f[:])
+        nc.vector.memset(zero[:], 0.0)
+        nc.vector.memset(w4s[:].rearrange("p g n -> p (g n)").bitcast(I32), 0)
+        nc.scalar.activation(out=warm[:], in_=zero[:], func=ACT.Silu)
+        nc.vector.tensor_copy(out=s_f[:], in_=s_bf[:])
+        x_transposes(0)
+        for n in range(WN_BUFS):
+            load_w(n)
+
+        mh_step = {}
+        for m in range(n_runs):
+            mh_step[m] = m + 2 if m < 4 else m + 3
+        mh_step[14] = 17
+        mh_step[15] = 17
+        last_step = 17
+
+        for j in range(-2, last_step + 1):
+            todo = pre_sched.get(j, [])
+            small = [n for n in todo if GROUPS[tiles[n][0]][2] == 1]
+            big = [n for n in todo if GROUPS[tiles[n][0]][2] == 2]
+
+            pre_items = []
+            for n in todo:
+                pre_items.append(lambda n=n: pre_a(n))
+                if n in small:
+                    pre_items.append(lambda n=n: pre_b_vector(n))
+                    pre_items.append(lambda n=n: load_w(n + WN_BUFS))
+            qw_items = []
+            if 0 <= j - 1 < n_runs:
+                qw_items = [lambda g=gq: quant_w(j - 1, g) for gq in range(5)]
+            ba_items = []
+            for m in range(n_runs):
+                if mh_step[m] == j + 1:
+                    ba_items.extend(basis_items(m))
+
+            if j == 1:
+                nc.vector.tensor_reduce(
+                    out=mask4[:], in_=ident_f[:].rearrange("p (m r) -> p r m", r=4), axis=AX.X, op=ALU.add
+                )
+                nc.vector.tensor_tensor(
+                    out=gm[:],
+                    in0=gridb[:].rearrange("p (a r) -> p a r", r=4),
+                    in1=mask4[:].unsqueeze(1).to_broadcast([P, 5, 4]),
+                    op=ALU.mult,
+                )
+                nc.vector.tensor_reduce(out=grid_f[:], in_=gm[:], axis=AX.X, op=ALU.add)
+            if j == 3:
+                base_quant(0)
+                base_quant(1)
+
+            for item in qw_items:
+                item()
+            if 0 <= j < n_runs:
+                half_run(j)
+            if j == 1:
+                x_transposes(1)
+                base_transposes(0)
+                base_transposes(1)
+            for item in weave((1.0, pre_items), (1.0, ba_items)):
+                item()
+            if j == 3:
+                base_matmuls()
+            for n in big:
+                pre_b_scalar(n)
+                load_w(n + WN_BUFS)
+
+            for m in range(n_runs - 2):
+                if mh_step[m] == j:
+                    for gq in gqs_of(m):
+                        for mt in range(4):
+                            mx_pass(m // 2, gq, mt)
+            if j == last_step:
+                for mt in range(4):
+                    for gq in range(5):
+                        mx_pass(7, gq, mt)
+                    finish(mt)

@@ -34,7 +34,6 @@ def tile_relukanlayer_kernel(
 ):
     nc = tc.nc
     with ExitStack() as ctx:
-        ctx.enter_context(tc.manual_schedule())
         const = ctx.enter_context(tc.tile_pool(name="const", bufs=1))
         wn_pool = ctx.enter_context(tc.tile_pool(name="wn", bufs=WN_BUFS))
         wp_pool = ctx.enter_context(tc.tile_pool(name="wp", bufs=16))

@@ -19,6 +19,11 @@ AX = mybir.AxisListType
 P = 128
 GROUPS = ((0, 0, 1), (0, 1, 1), (0, 2, 2), (1, 0, 2), (1, 2, 2))
 WN_BUFS = 8
+PER_CYCLE = 4
+MX_PER_CYCLE = 2
+MX_LAG = 2
+GRID_AT = 1
+BASE_AT = (2, 4)
 
 
 def weave(*weighted):
@@ -34,6 +39,7 @@ def tile_relukanlayer_kernel(
 ):
     nc = tc.nc
     with ExitStack() as ctx:
+        ctx.enter_context(tc.manual_schedule())
         const = ctx.enter_context(tc.tile_pool(name="const", bufs=1))
         wn_pool = ctx.enter_context(tc.tile_pool(name="wn", bufs=WN_BUFS))
         wp_pool = ctx.enter_context(tc.tile_pool(name="wp", bufs=16))
@@ -52,16 +58,6 @@ def tile_relukanlayer_kernel(
         tiles = [(gi, ob) for gi in range(len(GROUPS)) for ob in range(16)]
         runs = [(gi, h, cl2) for gi, grp in enumerate(GROUPS) for h in range(2) for cl2 in range(grp[2])]
         n_runs = len(runs)
-        pre_sched = {}
-        for r, (gi, h, cl2) in enumerate(runs):
-            if cl2 != 0:
-                continue
-            first = 16 * gi + 8 * h
-            if GROUPS[gi][2] == 1:
-                pre_sched[r - 2] = list(range(first, first + 8))
-            else:
-                pre_sched[r - 2] = list(range(first, first + 4))
-                pre_sched[r - 1] = list(range(first + 4, first + 8))
 
         ident_bf = const.tile([P, P], BF16, name="ident_bf")
         ident_f = const.tile([P, P], F32, name="ident_f")
@@ -88,6 +84,7 @@ def tile_relukanlayer_kernel(
         after_load = {}
         wp_t = {}
         wbf_t = {}
+        tp_t = {}
         wq_t = {}
         bas_t = {}
         bq_t = {}
@@ -133,19 +130,21 @@ def tile_relukanlayer_kernel(
             gi, h, cl2 = runs[r]
             return 4 * GROUPS[gi][0] + GROUPS[gi][1] + cl2
 
-        def half_run(r):
+        def unit(r, gq):
             gi, h, cl2 = runs[r]
             ni = 32 * GROUPS[gi][2]
-            for gq in range(5):
-                tp = tp_pool.tile([P, 1024], BF16, name="tp", tag="tp")
-                off = gq * ni * 4 + cl2 * P
-                for j in range(8):
-                    nc.tensor.transpose(
-                        tp[:, P * j : P * (j + 1)], wp_t[16 * gi + 8 * h + j][:, off : off + P], ident_bf[:]
-                    )
-                wbf = wbf_pool.tile([P, 1024], BF16, name="wbf", tag="wbf", align_bytes=64)
-                nc.scalar.copy(out=wbf[:], in_=tp[:])
-                wbf_t[(r, gq)] = wbf
+            tp = tp_pool.tile([P, 1024], BF16, name="tp", tag="tp")
+            off = gq * ni * 4 + cl2 * P
+            for j in range(8):
+                nc.tensor.transpose(
+                    tp[:, P * j : P * (j + 1)], wp_t[16 * gi + 8 * h + j][:, off : off + P], ident_bf[:]
+                )
+            tp_t[(r, gq)] = tp
+
+        def evacuate(r, gq):
+            wbf = wbf_pool.tile([P, 1024], BF16, name="wbf", tag="wbf", align_bytes=64)
+            nc.scalar.copy(out=wbf[:], in_=tp_t[(r, gq)][:])
+            wbf_t[(r, gq)] = wbf
 
         def quant_w(r, gq):
             h = runs[r][1]
@@ -194,17 +193,14 @@ def tile_relukanlayer_kernel(
                 stop=(s == 7 and gq == 4),
             )
 
-        def gqs_of(m):
-            return (0, 1, 2) if m % 2 == 0 else (3, 4)
-
-        def basis_items(m):
-            s = m // 2
-            gqs = gqs_of(m)
-            items = [lambda g=gqs[0]: basis(s, g)]
-            for k in range(1, len(gqs)):
-                items.append(lambda g=gqs[k]: basis(s, g))
-                items.append(lambda g=gqs[k - 1]: quant_b(s, g))
-            items.append(lambda g=gqs[-1]: quant_b(s, g))
+        def basis_items(groups):
+            items = []
+            for k, (s, g) in enumerate(groups):
+                items.append(lambda s=s, g=g: basis(s, g))
+                if k > 0:
+                    items.append(lambda s=groups[k - 1][0], g=groups[k - 1][1]: quant_b(s, g))
+            if groups:
+                items.append(lambda s=groups[-1][0], g=groups[-1][1]: quant_b(s, g))
             return items
 
         def load_xrep(s):
@@ -290,7 +286,6 @@ def tile_relukanlayer_kernel(
             nc.sync.dma_start(out=xn[:, :, 512 * c : 512 * (c + 1)], in_=x_v[:, :, 512 * c : 512 * (c + 1)])
 
         def load_base():
-            nc.sync.dma_start(out=gridb[:], in_=grid.partition_broadcast(P))
             nc.sync.dma_start(out=w4[:].bitcast(I32), in_=base_weight_words.bitcast(I32).rearrange("g p n -> p g n"))
             for q in range(4):
                 nc.sync.dma_start(
@@ -314,6 +309,7 @@ def tile_relukanlayer_kernel(
             out=s_bf[:],
             in_=spline_scale.rearrange("(op ob) a b -> op (ob a b)", ob=16).unsqueeze(1).to_broadcast([32, 4, 16]),
         )
+        nc.sync.dma_start(out=gridb[:], in_=grid.partition_broadcast(P))
         make_identity(nc, ident_bf[:])
         make_identity(nc, ident_f[:])
         nc.vector.memset(zero[:], 0.0)
@@ -324,14 +320,36 @@ def tile_relukanlayer_kernel(
         for n in range(WN_BUFS):
             load_w(n)
 
-        mh_step = {}
-        for m in range(n_runs):
-            mh_step[m] = m + 2 if m < 4 else m + 3
-        mh_step[14] = 17
-        mh_step[15] = 17
-        last_step = 17
+        units = [(r, gq) for r in range(n_runs) for gq in range(5)]
+        n_cycles = len(units) // PER_CYCLE
+        cycle_of_unit = dict((u, k // PER_CYCLE) for k, u in enumerate(units))
+        pre_sched = {}
+        blocks = []
+        for r, (gi, h, cl2) in enumerate(runs):
+            if cl2 == 0:
+                blocks.append((16 * gi + 8 * h, r, r + GROUPS[gi][2] - 1))
+        for b, (first, r_lo, r_hi) in enumerate(blocks):
+            stop = cycle_of_unit[(r_lo, 0)] - 1
+            start = cycle_of_unit[(blocks[b - 2][2], 4)] if b >= 2 else stop
+            start = max(start, stop - 2)
+            span = stop - start + 1
+            for k in range(8):
+                pre_sched[start + k * span // 8] = pre_sched.get(start + k * span // 8, []) + [first + k]
+        mx_sched = {}
+        cyc, used = 0, 0
+        for s in range(8):
+            r_last = max(r for r in range(n_runs) if slice_of(r) == s)
+            for gq in range(5):
+                first = cycle_of_unit[(r_last, gq)] + MX_LAG
+                if first > cyc:
+                    cyc, used = first, 0
+                elif used >= MX_PER_CYCLE:
+                    cyc, used = cyc + 1, 0
+                mx_sched[cyc] = mx_sched.get(cyc, []) + [(s, gq)]
+                used += 1
+        last_cycle = max(mx_sched)
 
-        for j in range(-2, last_step + 1):
+        for j in range(min(pre_sched), last_cycle + 1):
             todo = pre_sched.get(j, [])
             small = [n for n in todo if GROUPS[tiles[n][0]][2] == 1]
             big = [n for n in todo if GROUPS[tiles[n][0]][2] == 2]
@@ -342,15 +360,7 @@ def tile_relukanlayer_kernel(
                 if n in small:
                     pre_items.append(lambda n=n: pre_b_vector(n))
                     pre_items.append(lambda n=n: load_w(n + WN_BUFS))
-            qw_items = []
-            if 0 <= j - 1 < n_runs:
-                qw_items = [lambda g=gq: quant_w(j - 1, g) for gq in range(5)]
-            ba_items = []
-            for m in range(n_runs):
-                if mh_step[m] == j + 1:
-                    ba_items.extend(basis_items(m))
-
-            if j == 1:
+            if j == GRID_AT:
                 nc.vector.tensor_reduce(
                     out=mask4[:], in_=ident_f[:].rearrange("p (m r) -> p r m", r=4), axis=AX.X, op=ALU.add
                 )
@@ -361,33 +371,35 @@ def tile_relukanlayer_kernel(
                     op=ALU.mult,
                 )
                 nc.vector.tensor_reduce(out=grid_f[:], in_=gm[:], axis=AX.X, op=ALU.add)
-            if j == 3:
+            if j == BASE_AT[1]:
                 base_quant(0)
                 base_quant(1)
-
-            for item in qw_items:
-                item()
-            if 0 <= j < n_runs:
-                half_run(j)
-            if j == 1:
+            if 1 <= j <= n_cycles:
+                for r, gq in units[PER_CYCLE * (j - 1) : PER_CYCLE * j]:
+                    quant_w(r, gq)
+            if 0 <= j < n_cycles:
+                for r, gq in units[PER_CYCLE * j : PER_CYCLE * (j + 1)]:
+                    unit(r, gq)
+                for r, gq in units[PER_CYCLE * j : PER_CYCLE * (j + 1)]:
+                    evacuate(r, gq)
+            if j == BASE_AT[0]:
                 x_transposes(1)
                 base_transposes(0)
                 base_transposes(1)
-            for item in weave((1.0, pre_items), (1.0, ba_items)):
+            for item in weave((1.0, pre_items), (1.0, basis_items(mx_sched.get(j + 1, [])))):
                 item()
-            if j == 3:
+            if j == BASE_AT[1]:
                 base_matmuls()
             for n in big:
                 pre_b_scalar(n)
                 load_w(n + WN_BUFS)
-
-            for m in range(n_runs - 2):
-                if mh_step[m] == j:
-                    for gq in gqs_of(m):
-                        for mt in range(4):
-                            mx_pass(m // 2, gq, mt)
-            if j == last_step:
+            groups = mx_sched.get(j, [])
+            if j < last_cycle:
+                for s, gq in groups:
+                    for mt in range(4):
+                        mx_pass(s, gq, mt)
+            else:
                 for mt in range(4):
-                    for gq in range(5):
-                        mx_pass(7, gq, mt)
+                    for s, gq in groups:
+                        mx_pass(s, gq, mt)
                     finish(mt)

@@ -351,8 +351,8 @@ def tile_relukanlayer_kernel(
 
         for j in range(min(pre_sched), last_cycle + 1):
             todo = pre_sched.get(j, [])
-            small = [n for n in todo if GROUPS[tiles[n][0]][2] == 1]
-            big = [n for n in todo if GROUPS[tiles[n][0]][2] == 2]
+            small = todo
+            big = []
 
             pre_items = []
             for n in todo:

@@ -68,6 +68,7 @@ def tile_relukanlayer_kernel(
         gm = const.tile([P, 5, 4], F32, name="gm")
         grid_f = const.tile([P, 5], F32, name="grid_f")
         zero = const.tile([P, 2], F32, name="zero")
+        filler = const.tile([P, 512], BF16, name="filler")
         warm = const.tile([P, 2], F32, name="warm")
         w4 = const.tile([P, 2, 1024], U8, name="w4", align_bytes=64)
         w4s = const.tile([P, 2, 512], U8, name="w4s", align_bytes=64)
@@ -129,6 +130,10 @@ def tile_relukanlayer_kernel(
         def slice_of(r):
             gi, h, cl2 = runs[r]
             return 4 * GROUPS[gi][0] + GROUPS[gi][1] + cl2
+
+        def keep_warm(n):
+            for k in range(n):
+                nc.tensor.matmul(out=acc[3][:], lhsT=ident_bf[:], rhs=filler[:], start=True, stop=True)
 
         def unit(r, gq):
             gi, h, cl2 = runs[r]
@@ -316,6 +321,8 @@ def tile_relukanlayer_kernel(
         nc.vector.memset(w4s[:].rearrange("p g n -> p (g n)").bitcast(I32), 0)
         nc.scalar.activation(out=warm[:], in_=zero[:], func=ACT.Silu)
         nc.vector.tensor_copy(out=s_f[:], in_=s_bf[:])
+        nc.gpsimd.memset(filler[:], 0.0)
+        keep_warm(5)
         x_transposes(0)
         for n in range(WN_BUFS):
             load_w(n)
@@ -351,8 +358,8 @@ def tile_relukanlayer_kernel(
 
         for j in range(min(pre_sched), last_cycle + 1):
             todo = pre_sched.get(j, [])
-            small = todo
-            big = []
+            small = [n for n in todo if GROUPS[tiles[n][0]][2] == 1]
+            big = [n for n in todo if GROUPS[tiles[n][0]][2] == 2]
 
             pre_items = []
             for n in todo:
@@ -380,6 +387,8 @@ def tile_relukanlayer_kernel(
             if 0 <= j < n_cycles:
                 for r, gq in units[PER_CYCLE * j : PER_CYCLE * (j + 1)]:
                     unit(r, gq)
+                    if j < min(mx_sched):
+                        keep_warm(1)
                 for r, gq in units[PER_CYCLE * j : PER_CYCLE * (j + 1)]:
                     evacuate(r, gq)
             if j == BASE_AT[0]:

from contextlib import ExitStack

import concourse.mybir as mybir
from concourse.masks import make_identity

FLOPS = 2 * 512 * 512 * (20 * 1024 + 1024)

BF16 = mybir.dt.bfloat16
F32 = mybir.dt.float32
I32 = mybir.dt.int32
U8 = mybir.dt.uint8
U32 = mybir.dt.uint32
FP8X4 = mybir.dt.float8_e4m3fn_x4
FP4X4 = mybir.dt.float4_e2m1fn_x4
ALU = mybir.AluOpType
ACT = mybir.ActivationFunctionType
AX = mybir.AxisListType

P = 128
GROUPS = ((0, 0, 1), (0, 1, 1), (0, 2, 2), (1, 0, 2), (1, 2, 2))
WN_BUFS = 8
PER_CYCLE = 4
MX_PER_CYCLE = 2
MX_LAG = 2
GRID_AT = 1
BASE_AT = (2, 4)


def weave(*weighted):
    keyed = []
    for li, (span, items) in enumerate(weighted):
        for k, item in enumerate(items):
            keyed.append(((k + 0.5) * span / len(items), li, k, item))
    return [entry[3] for entry in sorted(keyed, key=lambda e: (e[0], e[1], e[2]))]


def tile_relukanlayer_kernel(
    tc, x, base_weight_words, base_weight_scales, spline_weight, spline_scale, grid, out
):
    nc = tc.nc
    with ExitStack() as ctx:
        ctx.enter_context(tc.manual_schedule())
        const = ctx.enter_context(tc.tile_pool(name="const", bufs=1))
        wn_pool = ctx.enter_context(tc.tile_pool(name="wn", bufs=WN_BUFS))
        wp_pool = ctx.enter_context(tc.tile_pool(name="wp", bufs=16))
        wbf_pool = ctx.enter_context(tc.tile_pool(name="wbf", bufs=8))
        wq_pool = ctx.enter_context(tc.tile_pool(name="wq", bufs=3))
        bas_pool = ctx.enter_context(tc.tile_pool(name="bas", bufs=3))
        bq_pool = ctx.enter_context(tc.tile_pool(name="bq", bufs=2))
        res_pool = ctx.enter_context(tc.tile_pool(name="res", bufs=2))
        acc_pool = ctx.enter_context(tc.psum_pool(name="acc", bufs=1))
        tp_pool = ctx.enter_context(tc.psum_pool(name="tp", bufs=4))

        w_v = spline_weight.rearrange("(op ob) (c t r) g -> ob c op t (r g)", ob=16, c=2, t=4)
        x_v = x.rearrange("(m p) i -> p m i", p=P)
        scr = out.rearrange("(c r a) n -> c r (a n)", c=2, a=2)

        tiles = [(gi, ob) for gi in range(len(GROUPS)) for ob in range(16)]
        runs = [(gi, h, cl2) for gi, grp in enumerate(GROUPS) for h in range(2) for cl2 in range(grp[2])]
        n_runs = len(runs)

        ident_bf = const.tile([P, P], BF16, name="ident_bf")
        ident_f = const.tile([P, P], F32, name="ident_f")
        s_bf = const.tile([P, 16], BF16, name="s_bf")
        s_f = const.tile([P, 16], F32, name="s_f")
        gridb = const.tile([P, 20], BF16, name="gridb")
        mask4 = const.tile([P, 4], F32, name="mask4")
        gm = const.tile([P, 5, 4], F32, name="gm")
        grid_f = const.tile([P, 5], F32, name="grid_f")
        zero = const.tile([P, 2], F32, name="zero")
        filler = const.tile([P, 512], BF16, name="filler")
        warm = const.tile([P, 2], F32, name="warm")
        w4 = const.tile([P, 2, 1024], U8, name="w4", align_bytes=64)
        w4s = const.tile([P, 2, 512], U8, name="w4s", align_bytes=64)
        silq = const.tile([P, 2, 512], U32, name="silq", align_bytes=64)
        sils = const.tile([P, 2, 512], U8, name="sils", align_bytes=64)
        base_sb = const.tile([P, 4, 512], F32, name="base_sb")
        xn = const.tile([P, 4, 1024], BF16, name="xn")
        xt4 = const.tile([P, 2, 512, 4], BF16, name="xt4")
        sil = const.tile([P, 2, 512, 4], BF16, name="sil", align_bytes=64)
        xrep = [const.tile([P, 2048], BF16, name="xrep%d" % s) for s in range(8)]
        acc = [acc_pool.tile([P, 512], F32, name="acc%d" % mt) for mt in range(4)]

        wn_t = {}
        after_load = {}
        wp_t = {}
        wbf_t = {}
        tp_t = {}
        wq_t = {}
        bas_t = {}
        bq_t = {}

        def load_w(n):
            if n >= len(tiles):
                return
            gi, ob = tiles[n]
            c, cl0, ncl = GROUPS[gi]
            wn = wn_pool.tile([P, 1280], BF16, name="wn", tag="wn")
            nc.sync.dma_start(out=wn[:, : 640 * ncl], in_=w_v[ob, c][:, :, 640 * cl0 : 640 * (cl0 + ncl)])
            wn_t[n] = wn
            for extra in after_load.get(n, []):
                extra()

        def pre_views(n):
            ncl = GROUPS[tiles[n][0]][2]
            src = wn_t[n][:, : 640 * ncl].rearrange("q (i a b) -> q a i b", a=5, b=4)
            dst = wp_t[n][:, : 640 * ncl].rearrange("q (a i b) -> q a i b", a=5, b=4)
            return src, dst

        def pre_a(n):
            wp_t[n] = wp_pool.tile([P, 1280], BF16, name="wp", tag="wp")
            src, dst = pre_views(n)
            ob = tiles[n][1]
            nc.vector.tensor_scalar(
                out=dst[:, 0:4], in0=src[:, 0:4], scalar1=s_f[:, ob : ob + 1], scalar2=None, op0=ALU.mult
            )

        def pre_b_vector(n):
            src, dst = pre_views(n)
            ob = tiles[n][1]
            nc.vector.tensor_scalar(
                out=dst[:, 4], in0=src[:, 4], scalar1=s_f[:, ob : ob + 1], scalar2=None, op0=ALU.mult
            )

        def pre_b_scalar(n):
            src, dst = pre_views(n)
            ob = tiles[n][1]
            nc.scalar.activation(out=dst[:, 4], in_=src[:, 4], func=ACT.Copy, scale=s_f[:, ob : ob + 1])

        def slice_of(r):
            gi, h, cl2 = runs[r]
            return 4 * GROUPS[gi][0] + GROUPS[gi][1] + cl2

        def keep_warm(n):
            for k in range(n):
                nc.tensor.matmul(out=acc[3][:], lhsT=ident_bf[:], rhs=filler[:], start=True, stop=True)

        def unit(r, gq):
            gi, h, cl2 = runs[r]
            ni = 32 * GROUPS[gi][2]
            tp = tp_pool.tile([P, 1024], BF16, name="tp", tag="tp")
            off = gq * ni * 4 + cl2 * P
            for j in range(8):
                nc.tensor.transpose(
                    tp[:, P * j : P * (j + 1)], wp_t[16 * gi + 8 * h + j][:, off : off + P], ident_bf[:]
                )
            tp_t[(r, gq)] = tp

        def evacuate(r, gq):
            wbf = wbf_pool.tile([P, 1024], BF16, name="wbf", tag="wbf", align_bytes=64)
            nc.scalar.copy(out=wbf[:], in_=tp_t[(r, gq)][:])
            wbf_t[(r, gq)] = wbf

        def quant_w(r, gq):
            h = runs[r][1]
            s = slice_of(r)
            if s not in wq_t:
                wq_t[s] = (
                    wq_pool.tile([P, 5, 512], U32, name="wq", tag="wq", align_bytes=64),
                    wq_pool.tile([P, 5, 512], U8, name="wsc", tag="wsc", align_bytes=64),
                )
            codes, scales = wq_t[s]
            nc.vector.quantize_mx(
                out=codes[:, gq, 256 * h : 256 * (h + 1)].bitcast(FP8X4),
                scales=scales[:, gq, 256 * h : 256 * (h + 1)],
                in_=wbf_t[(r, gq)][:],
            )

        def basis(s, gq):
            bas = bas_pool.tile([P, 2048], BF16, name="bas", tag="bas", align_bytes=64)
            nc.vector.tensor_scalar(
                out=bas[:],
                in0=xrep[s][:],
                scalar1=grid_f[:, gq : gq + 1],
                scalar2=0.0,
                op0=ALU.subtract,
                op1=ALU.max,
            )
            bas_t[(s, gq)] = bas

        def quant_b(s, gq):
            if s not in bq_t:
                bq_t[s] = (
                    bq_pool.tile([P, 5, 512], U32, name="bq", tag="bq", align_bytes=64),
                    bq_pool.tile([P, 5, 512], U8, name="bsc", tag="bsc", align_bytes=64),
                )
            codes, scales = bq_t[s]
            nc.vector.quantize_mx(out=codes[:, gq, :].bitcast(FP8X4), scales=scales[:, gq, :], in_=bas_t[(s, gq)][:])

        def mx_pass(s, gq, mt):
            nc.tensor.matmul_mx(
                out=acc[mt][:],
                lhsT=bq_t[s][0][:, gq, P * mt : P * (mt + 1)].bitcast(FP8X4),
                lhsT_scale=bq_t[s][1][:, gq, P * mt : P * (mt + 1)],
                rhs=wq_t[s][0][:, gq, :].bitcast(FP8X4),
                rhs_scale=wq_t[s][1][:, gq, :],
                start=(s == 0 and gq == 0),
                stop=(s == 7 and gq == 4),
            )

        def basis_items(groups):
            items = []
            for k, (s, g) in enumerate(groups):
                items.append(lambda s=s, g=g: basis(s, g))
                if k > 0:
                    items.append(lambda s=groups[k - 1][0], g=groups[k - 1][1]: quant_b(s, g))
            if groups:
                items.append(lambda s=groups[-1][0], g=groups[-1][1]: quant_b(s, g))
            return items

        def load_xrep(s):
            c, cl = s // 4, s % 4
            nc.sync.dma_start(
                out=xrep[s][:].bitcast(F32),
                in_=scr[c][32 * cl : 32 * (cl + 1), :].unsqueeze(1).to_broadcast([32, 4, 1024]),
            )

        def x_transposes(c):
            for mp in range(2):
                tp = tp_pool.tile([P, 1024], BF16, name="tp", tag="tp")
                for m2 in range(2):
                    for t in range(4):
                        k = 4 * m2 + t
                        nc.tensor.transpose(
                            tp[:, P * k : P * (k + 1)],
                            xn[:, 2 * mp + m2, 512 * c + P * t : 512 * c + P * (t + 1)],
                            ident_bf[:],
                        )
                nc.scalar.copy(
                    out=xt4[:, c, 256 * mp : 256 * (mp + 1), :].rearrange("p (m b) t -> p m b t", m=2),
                    in_=tp[:].rearrange("p (m t b) -> p m b t", m=2, t=4),
                )

        def store_xt(c):
            nc.sync.dma_start(out=scr[c], in_=xt4[:, c].rearrange("p b t -> p (b t)").bitcast(F32))

        def base_transposes(c):
            for mp in range(2):
                tpf = tp_pool.tile([P, 512], F32, name="tpf", tag="tp")
                for m2 in range(2):
                    words = xn[:, 2 * mp + m2, :].bitcast(F32)
                    for u in range(2):
                        k = 2 * m2 + u
                        nc.tensor.transpose(
                            tpf[:, P * k : P * (k + 1)], words[:, 256 * c + u : 256 * (c + 1) : 2], ident_f[:]
                        )
                for m2 in range(2):
                    mt = 2 * mp + m2
                    nc.scalar.activation(
                        out=sil[:, c, P * mt : P * (mt + 1), :].rearrange("p b (u e) -> p b u e", u=2),
                        in_=tpf[:, 256 * m2 : 256 * (m2 + 1)].bitcast(BF16).rearrange("p (u b e) -> p b u e", u=2, e=2),
                        func=ACT.Silu,
                    )

        def base_quant(c):
            nc.vector.quantize_mx(
                out=silq[:, c, :].bitcast(FP8X4),
                scales=sils[:, c, :],
                in_=sil[:, c].rearrange("p b t -> p (b t)"),
            )

        def base_matmuls():
            for mt in range(4):
                pb = tp_pool.tile([P, 512], F32, name="pb", tag="tp")
                for c in range(2):
                    nc.tensor.matmul_mx(
                        out=pb[:],
                        lhsT=silq[:, c, P * mt : P * (mt + 1)].bitcast(FP8X4),
                        lhsT_scale=sils[:, c, P * mt : P * (mt + 1)],
                        rhs=w4[:, c, :].bitcast(FP4X4),
                        rhs_scale=w4s[:, c, :],
                        start=(c == 0),
                        stop=(c == 1),
                    )
                if mt % 2 == 0:
                    nc.scalar.copy(out=base_sb[:, mt, :], in_=pb[:])
                else:
                    nc.vector.tensor_copy(out=base_sb[:, mt, :], in_=pb[:])

        def finish(mt):
            res = res_pool.tile([P, 512], F32, name="res", tag="res")
            nc.vector.tensor_tensor(
                out=res[:].rearrange("b (op ob) -> b op ob", ob=16),
                in0=acc[mt][:].rearrange("b (ob op) -> b op ob", ob=16),
                in1=base_sb[:, mt, :].rearrange("b (op ob) -> b op ob", ob=16),
                op=ALU.add,
            )
            nc.sync.dma_start(out=out[P * mt : P * (mt + 1), :], in_=res[:])

        def load_x(c):
            nc.sync.dma_start(out=xn[:, :, 512 * c : 512 * (c + 1)], in_=x_v[:, :, 512 * c : 512 * (c + 1)])

        def load_base():
            nc.sync.dma_start(out=w4[:].bitcast(I32), in_=base_weight_words.bitcast(I32).rearrange("g p n -> p g n"))
            for q in range(4):
                nc.sync.dma_start(
                    out=w4s[32 * q : 32 * q + 4].bitcast(I32),
                    in_=base_weight_scales.bitcast(I32)[:, 4 * q : 4 * q + 4, :].rearrange("g r n -> r g n"),
                )

        after_load[15] = [lambda: store_xt(0), lambda: load_x(1)]
        after_load[23] = [lambda: load_xrep(0)]
        after_load[27] = [load_base]
        after_load[31] = [lambda: load_xrep(1)]
        after_load[35] = [lambda: store_xt(1), lambda: load_xrep(2)]
        after_load[39] = [lambda: load_xrep(3)]
        after_load[43] = [lambda: load_xrep(4)]
        after_load[47] = [lambda: load_xrep(5)]
        after_load[51] = [lambda: load_xrep(6)]
        after_load[55] = [lambda: load_xrep(7)]

        load_x(0)
        nc.sync.dma_start(
            out=s_bf[:],
            in_=spline_scale.rearrange("(op ob) a b -> op (ob a b)", ob=16).unsqueeze(1).to_broadcast([32, 4, 16]),
        )
        nc.sync.dma_start(out=gridb[:], in_=grid.partition_broadcast(P))
        make_identity(nc, ident_bf[:])
        make_identity(nc, ident_f[:])
        nc.vector.memset(zero[:], 0.0)
        nc.vector.memset(w4s[:].rearrange("p g n -> p (g n)").bitcast(I32), 0)
        nc.scalar.activation(out=warm[:], in_=zero[:], func=ACT.Silu)
        nc.vector.tensor_copy(out=s_f[:], in_=s_bf[:])
        nc.gpsimd.memset(filler[:], 0.0)
        keep_warm(5)
        x_transposes(0)
        for n in range(WN_BUFS):
            load_w(n)

        units = [(r, gq) for r in range(n_runs) for gq in range(5)]
        n_cycles = len(units) // PER_CYCLE
        cycle_of_unit = dict((u, k // PER_CYCLE) for k, u in enumerate(units))
        pre_sched = {}
        blocks = []
        for r, (gi, h, cl2) in enumerate(runs):
            if cl2 == 0:
                blocks.append((16 * gi + 8 * h, r, r + GROUPS[gi][2] - 1))
        for b, (first, r_lo, r_hi) in enumerate(blocks):
            stop = cycle_of_unit[(r_lo, 0)] - 1
            start = cycle_of_unit[(blocks[b - 2][2], 4)] if b >= 2 else stop
            start = max(start, stop - 2)
            span = stop - start + 1
            for k in range(8):
                pre_sched[start + k * span // 8] = pre_sched.get(start + k * span // 8, []) + [first + k]
        mx_sched = {}
        cyc, used = 0, 0
        for s in range(8):
            r_last = max(r for r in range(n_runs) if slice_of(r) == s)
            for gq in range(5):
                first = cycle_of_unit[(r_last, gq)] + MX_LAG
                if first > cyc:
                    cyc, used = first, 0
                elif used >= MX_PER_CYCLE:
                    cyc, used = cyc + 1, 0
                mx_sched[cyc] = mx_sched.get(cyc, []) + [(s, gq)]
                used += 1
        last_cycle = max(mx_sched)

        for j in range(min(pre_sched), last_cycle + 1):
            todo = pre_sched.get(j, [])
            small = [n for n in todo if GROUPS[tiles[n][0]][2] == 1]
            big = [n for n in todo if GROUPS[tiles[n][0]][2] == 2]

            pre_items = []
            for n in todo:
                pre_items.append(lambda n=n: pre_a(n))
                if n in small:
                    pre_items.append(lambda n=n: pre_b_vector(n))
                    pre_items.append(lambda n=n: load_w(n + WN_BUFS))
            if j == GRID_AT:
                nc.vector.tensor_reduce(
                    out=mask4[:], in_=ident_f[:].rearrange("p (m r) -> p r m", r=4), axis=AX.X, op=ALU.add
                )
                nc.vector.tensor_tensor(
                    out=gm[:],
                    in0=gridb[:].rearrange("p (a r) -> p a r", r=4),
                    in1=mask4[:].unsqueeze(1).to_broadcast([P, 5, 4]),
                    op=ALU.mult,
                )
                nc.vector.tensor_reduce(out=grid_f[:], in_=gm[:], axis=AX.X, op=ALU.add)
            if j == BASE_AT[1]:
                base_quant(0)
                base_quant(1)
            if 1 <= j <= n_cycles:
                for r, gq in units[PER_CYCLE * (j - 1) : PER_CYCLE * j]:
                    quant_w(r, gq)
            if 0 <= j < n_cycles:
                for r, gq in units[PER_CYCLE * j : PER_CYCLE * (j + 1)]:
                    unit(r, gq)
                    if j < min(mx_sched):
                        keep_warm(1)
                for r, gq in units[PER_CYCLE * j : PER_CYCLE * (j + 1)]:
                    evacuate(r, gq)
            if j == BASE_AT[0]:
                x_transposes(1)
                base_transposes(0)
                base_transposes(1)
            for item in weave((1.0, pre_items), (1.0, basis_items(mx_sched.get(j + 1, [])))):
                item()
            if j == BASE_AT[1]:
                base_matmuls()
            for n in big:
                pre_b_scalar(n)
                load_w(n + WN_BUFS)
            groups = mx_sched.get(j, [])
            if j < last_cycle:
                for s, gq in groups:
                    for mt in range(4):
                        mx_pass(s, gq, mt)
            else:
                for mt in range(4):
                    for s, gq in groups:
                        mx_pass(s, gq, mt)
                    finish(mt)
